import numpy as np
import ml_dtypes


def mxq(x, axis, fmt="e4m3"):
    dtype, down = {"e4m3": (ml_dtypes.float8_e4m3fn, 7), "e5m2": (ml_dtypes.float8_e5m2, 14)}[fmt]
    v = np.moveaxis(np.asarray(x, np.float32).astype(ml_dtypes.bfloat16).astype(np.float64), axis, -1)
    blocks = v.reshape(v.shape[:-1] + (-1, 32))
    amax = np.abs(blocks).max(-1, keepdims=True)
    byte = np.maximum(np.where(amax > 0, np.frexp(amax)[1] - 1 + 127, 0) - down, 1)
    scale = np.exp2(byte - 127.0)
    codes = (blocks / scale).astype(np.float32).astype(dtype).astype(np.float64)
    return np.moveaxis((codes * scale).reshape(v.shape), -1, axis)


WIDE = False


def mx_kscale(k):
    if not WIDE:
        return np.ones(k)
    levels = np.array([10, -10, 5, -5, 0])
    a = np.random.permutation(np.resize(levels, k // 512 * 4)).reshape(k // 512, 4)
    idx = np.arange(k)
    return np.exp2(a[idx // 512, idx % 128 // 32])


BF16 = ml_dtypes.bfloat16


def bf(x):
    return np.asarray(x, np.float32).astype(BF16)


def f64(x):
    return np.asarray(x).astype(np.float64)


B, S, D, H, DH, F = 1, 256, 1024, 8, 128, 4096
INNER = H * DH
HALF = DH // 2
EPS = 1e-5


def rmsnorm(u, g):
    var = np.mean(np.square(u), axis=-1, keepdims=True)
    return u * (1.0 / np.sqrt(var + EPS)) * g


def rope_interleaved(u, cos, sin):
    u1 = u[..., 0::2]
    u2 = u[..., 1::2]
    c = cos[None, :, None, :]
    s = sin[None, :, None, :]
    o1 = u1 * c - u2 * s
    o2 = u2 * c + u1 * s
    return np.stack([o1, o2], axis=-1).reshape(u.shape)


def setup_inputs():
    s = mx_kscale(D)
    ang = np.random.uniform(0.0, 2.0 * np.pi, (S, HALF))
    return {"hidden_states": bf(np.random.standard_normal((B, S, D)) * s),
            "w_q": bf(np.random.standard_normal((D, INNER)) * 0.02 / np.sqrt(D) / s[:, None]),
            "w_k": bf(np.random.standard_normal((D, INNER)) * 0.02 / np.sqrt(D) / s[:, None]),
            "w_v": bf(np.random.standard_normal((D, INNER)) * 3.0 / np.sqrt(D) / s[:, None]),
            "norm_q_w": bf(1.0 + 0.1 * np.random.standard_normal(DH)),
            "norm_k_w": bf(1.0 + 0.1 * np.random.standard_normal(DH)),
            "cos": bf(np.cos(ang)),
            "sin": bf(np.sin(ang))}


def reference(hidden_states, w_q, w_k, w_v, norm_q_w, norm_k_w, cos, sin):
    xq = mxq(f64(hidden_states), 2, "e4m3")
    q = (xq @ mxq(f64(w_q), 0, "e4m3")).reshape(B, S, H, DH)
    k = (xq @ mxq(f64(w_k), 0, "e4m3")).reshape(B, S, H, DH)
    v = (xq @ mxq(f64(w_v), 0, "e4m3")).reshape(B, S, H, DH)
    q = rmsnorm(q, f64(norm_q_w))
    k = rmsnorm(k, f64(norm_k_w))
    q = rope_interleaved(q, f64(cos), f64(sin))
    k = rope_interleaved(k, f64(cos), f64(sin))
    return q, k, v

@@ -1,0 +1,259 @@
+from contextlib import ExitStack
+
+import concourse.mybir as mybir
+from concourse.masks import make_identity
+
+F32 = mybir.dt.float32
+BF16 = mybir.dt.bfloat16
+U32 = mybir.dt.uint32
+U8 = mybir.dt.uint8
+FP8X4 = mybir.dt.float8_e4m3fn_x4
+ACT = mybir.ActivationFunctionType
+ALU = mybir.AluOpType
+
+P = 128
+PACK = 4
+K_PASS = P * PACK
+TOKENS = 256
+D_MODEL = 1024
+INNER = 1024
+HEAD = 128
+HALF = HEAD // 2
+EPS = 1e-5
+BANK = 512
+TOKEN_TILES = TOKENS // P
+PASSES = D_MODEL // K_PASS
+BANKS = INNER // BANK
+HEADS_PER_BANK = BANK // HEAD
+HEADS = INNER // HEAD
+NORMED = 2
+SLABS = 3 * PASSES
+RUN = 4
+SCALAR_COLS = 640
+
+FLOPS = 2 * TOKENS * D_MODEL * 3 * INNER
+
+
+def tile_flux2parallelselfattention_pa_kernel(
+    tc, hidden_states, w_q, w_k, w_v, norm_q_w, norm_k_w, cos, sin, out_0, out_1, out_2
+):
+    nc = tc.nc
+    weights = [w_q, w_k, w_v]
+    gains = [norm_q_w, norm_k_w]
+    outs = [o.rearrange("b s h d -> (b s) (h d)") for o in (out_0, out_1, out_2)]
+    x_rows = hidden_states.rearrange("b s k -> (b s) k")
+
+    with ExitStack() as ctx:
+        keep = ctx.enter_context(tc.tile_pool(name="keep", bufs=1))
+        stage = ctx.enter_context(tc.tile_pool(name="stage", bufs=3))
+        work = ctx.enter_context(tc.tile_pool(name="work", bufs=2))
+        psum = ctx.enter_context(tc.psum_pool(name="psum", bufs=8))
+
+        raw = [keep.tile([P, PACK, INNER], BF16, name="raw%d" % j) for j in range(SLABS)]
+
+        def load_slab(j):
+            w, c = divmod(j, PASSES)
+            rows = weights[w][c * K_PASS : (c + 1) * K_PASS, :]
+            nc.sync.dma_start(out=raw[j][:], in_=rows.rearrange("(p t) n -> p t n", t=PACK))
+
+        x_sb = keep.tile([P, TOKEN_TILES * D_MODEL], BF16)
+        cos_sb = keep.tile([P, TOKEN_TILES, HALF], BF16)
+        sin_sb = keep.tile([P, TOKEN_TILES, HALF], BF16)
+        gain_sb = keep.tile([P, NORMED, HEAD], BF16)
+
+        load_slab(0)
+        nc.sync.dma_start(
+            out=x_sb[:].rearrange("p (a k) -> p a k", a=TOKEN_TILES),
+            in_=x_rows.rearrange("(a p) k -> p a k", p=P),
+        )
+        load_slab(1)
+        nc.sync.dma_start(out=cos_sb[:], in_=cos.rearrange("(a p) i -> p a i", p=P))
+        nc.sync.dma_start(out=sin_sb[:], in_=sin.rearrange("(a p) i -> p a i", p=P))
+        for w in range(NORMED):
+            nc.sync.dma_start(out=gain_sb[:, w, :], in_=gains[w].partition_broadcast(P))
+        for j in range(2, SLABS):
+            load_slab(j)
+
+        ident = keep.tile([P, P], F32)
+        make_identity(nc, ident[:])
+        eps_sb = keep.tile([P, 1], F32)
+        nc.vector.memset(eps_sb[:], EPS)
+        warm = keep.tile([P, 1], F32)
+        nc.scalar.activation(out=warm[:], in_=eps_sb[:], func=ACT.Sqrt)
+
+        w_codes = keep.tile([P, SLABS, INNER], U32, align_bytes=64)
+        w_scales = keep.tile([P, SLABS, INNER], U8, align_bytes=64)
+        grouped_of = {}
+
+        def regroup(j):
+            grouped = stage.tile([P, INNER, PACK], BF16, align_bytes=64)
+            dst = grouped[:].rearrange("p (g i) t -> p g t i", i=RUN)
+            src = raw[j][:].rearrange("p t (g i) -> p g t i", i=RUN)
+            split = SCALAR_COLS // RUN
+            nc.scalar.copy(out=dst[:, :split], in_=src[:, :split])
+            nc.vector.tensor_copy(out=dst[:, split:], in_=src[:, split:])
+            grouped_of[j] = grouped
+
+        def quantise(j):
+            nc.vector.quantize_mx(
+                out=w_codes[:, j, :].bitcast(FP8X4),
+                scales=w_scales[:, j, :],
+                in_=grouped_of[j][:].rearrange("p n t -> p (n t)"),
+            )
+
+        x_words = x_sb[:].bitcast(F32).rearrange(
+            "s (a c q u) -> s a c u q", a=TOKEN_TILES, c=PASSES, q=P, u=2
+        )
+        x_grouped = keep.tile([P, PASSES * TOKENS * PACK], BF16, align_bytes=64)
+        x_grouped_words = x_grouped[:].bitcast(F32).rearrange(
+            "p (c a s u) -> p c a s u", c=PASSES, a=TOKEN_TILES, s=P, u=2
+        )
+        x_codes = keep.tile([P, PASSES * TOKENS], U32, align_bytes=64)
+        x_scales = keep.tile([P, PASSES * TOKENS], U8, align_bytes=64)
+
+        def transpose_x():
+            for a in range(TOKEN_TILES):
+                x_t = psum.tile([P, PASSES, 2, P], F32, tag="bank")
+                for c in range(PASSES):
+                    for u in range(2):
+                        nc.tensor.transpose(
+                            out=x_t[:, c, u, :], in_=x_words[:, a, c, u, :], identity=ident[:]
+                        )
+                nc.vector.tensor_copy(
+                    out=x_grouped_words[:, :, a, :, :], in_=x_t[:].rearrange("p c u s -> p c s u")
+                )
+
+        def quantise_x():
+            nc.vector.quantize_mx(
+                out=x_codes[:].bitcast(FP8X4), scales=x_scales[:], in_=x_grouped[:]
+            )
+
+        acc_of = {}
+
+        def multiply(j):
+            w, c = divmod(j, PASSES)
+            for a in range(TOKEN_TILES):
+                x_cols = slice((c * TOKEN_TILES + a) * P, (c * TOKEN_TILES + a + 1) * P)
+                for b in range(BANKS):
+                    n_cols = slice(b * BANK, (b + 1) * BANK)
+                    if c == 0:
+                        acc_of[(w, a, b)] = psum.tile([P, BANK], F32, tag="bank", name="acc")
+                    nc.tensor.matmul_mx(
+                        out=acc_of[(w, a, b)][:],
+                        lhsT=x_codes[:, x_cols].bitcast(FP8X4),
+                        lhsT_scale=x_scales[:, x_cols],
+                        rhs=w_codes[:, j, n_cols].bitcast(FP8X4),
+                        rhs_scale=w_scales[:, j, n_cols],
+                        start=(c == 0),
+                        stop=(c == PASSES - 1),
+                    )
+
+        cos_gain = [keep.tile([P, TOKEN_TILES, HALF, 2], F32, name="cos_gain%d" % w) for w in range(NORMED)]
+        sin_gain = [keep.tile([P, TOKEN_TILES, 2, HALF], F32, name="sin_gain%d" % w) for w in range(NORMED)]
+
+        def build_tables():
+            neg_sin = keep.tile([P, TOKEN_TILES, HALF], BF16)
+            nc.vector.tensor_scalar_mul(out=neg_sin[:], in0=sin_sb[:], scalar1=-1.0)
+            for w in range(NORMED):
+                gain_pairs = gain_sb[:, w, :].rearrange("p (i e) -> p i e", e=2)
+                nc.vector.tensor_tensor(
+                    out=cos_gain[w][:],
+                    in0=cos_sb[:].unsqueeze(3).to_broadcast([P, TOKEN_TILES, HALF, 2]),
+                    in1=gain_pairs.unsqueeze(1).to_broadcast([P, TOKEN_TILES, HALF, 2]),
+                    op=ALU.mult,
+                )
+                nc.vector.tensor_tensor(
+                    out=sin_gain[w][:, :, 0, :],
+                    in0=neg_sin[:],
+                    in1=gain_pairs[:, :, 1].unsqueeze(1).to_broadcast([P, TOKEN_TILES, HALF]),
+                    op=ALU.mult,
+                )
+                nc.vector.tensor_tensor(
+                    out=sin_gain[w][:, :, 1, :],
+                    in0=sin_sb[:],
+                    in1=gain_pairs[:, :, 0].unsqueeze(1).to_broadcast([P, TOKEN_TILES, HALF]),
+                    op=ALU.mult,
+                )
+
+        def norm_and_rotate(w, a):
+            squares = work.tile([P, INNER], F32)
+            sum_sq = work.tile([P, HEADS], F32)
+            for b in range(BANKS):
+                for h in range(HEADS_PER_BANK):
+                    head = b * HEADS_PER_BANK + h
+                    nc.scalar.activation(
+                        out=squares[:, head * HEAD : (head + 1) * HEAD],
+                        in_=acc_of[(w, a, b)][:, h * HEAD : (h + 1) * HEAD],
+                        func=ACT.Square,
+                        accum_out=sum_sq[:, head : head + 1],
+                    )
+            rms = work.tile([P, HEADS], F32)
+            nc.scalar.activation(
+                out=rms[:], in_=sum_sq[:], func=ACT.Sqrt, bias=eps_sb[:, 0:1], scale=1.0 / HEAD
+            )
+
+            direct = work.tile([P, INNER], F32)
+            cross = work.tile([P, BANKS, 2, BANK // 2], F32)
+            for b in range(BANKS):
+                acc = acc_of[(w, a, b)]
+                acc_pairs = acc[:].rearrange("p (n e) -> p e n", e=2)
+                for e in range(2):
+                    nc.vector.tensor_tensor(
+                        out=cross[:, b, e, :].rearrange("p (h i) -> p h i", h=HEADS_PER_BANK),
+                        in0=acc_pairs[:, 1 - e, :].rearrange("p (h i) -> p h i", h=HEADS_PER_BANK),
+                        in1=sin_gain[w][:, a, e, :].unsqueeze(1).to_broadcast([P, HEADS_PER_BANK, HALF]),
+                        op=ALU.mult,
+                    )
+                nc.vector.tensor_tensor(
+                    out=direct[:, b * BANK : (b + 1) * BANK].rearrange("p (h d) -> p h d", h=HEADS_PER_BANK),
+                    in0=acc[:].rearrange("p (h d) -> p h d", h=HEADS_PER_BANK),
+                    in1=cos_gain[w][:, a, :, :]
+                    .rearrange("p i e -> p (i e)")
+                    .unsqueeze(1)
+                    .to_broadcast([P, HEADS_PER_BANK, HEAD]),
+                    op=ALU.mult,
+                )
+            direct_pairs = direct[:].rearrange("p (b n e) -> p b n e", b=BANKS, e=2)
+            nc.vector.tensor_tensor(
+                out=direct_pairs, in0=direct_pairs, in1=cross[:].rearrange("p b e n -> p b n e"), op=ALU.add
+            )
+            inv_rms = work.tile([P, HEADS], F32)
+            nc.vector.reciprocal(out=inv_rms[:], in_=rms[:])
+
+            rotated = work.tile([P, INNER], F32)
+            for head in range(HEADS):
+                cols = slice(head * HEAD, (head + 1) * HEAD)
+                nc.scalar.activation(
+                    out=rotated[:, cols], in_=direct[:, cols], func=ACT.Copy, scale=inv_rms[:, head : head + 1]
+                )
+            nc.sync.dma_start(out=outs[w][a * P : (a + 1) * P, :], in_=rotated[:])
+
+        def store_v():
+            w = NORMED
+            for a in range(TOKEN_TILES):
+                for b in range(BANKS):
+                    plain = work.tile([P, BANK], F32, bufs=TOKEN_TILES * BANKS)
+                    if b % 2 == 0:
+                        nc.scalar.copy(out=plain[:], in_=acc_of[(w, a, b)][:])
+                    else:
+                        nc.vector.tensor_copy(out=plain[:], in_=acc_of[(w, a, b)][:])
+                    nc.sync.dma_start(
+                        out=outs[w][a * P : (a + 1) * P, b * BANK : (b + 1) * BANK], in_=plain[:]
+                    )
+
+        regroup(0)
+        transpose_x()
+        regroup(1)
+        quantise_x()
+        quantise(0)
+        multiply(0)
+        build_tables()
+        for j in range(1, SLABS):
+            if j + 1 < SLABS:
+                regroup(j + 1)
+            quantise(j)
+            multiply(j)
+            if j >= PASSES:
+                w, a = divmod(j - PASSES, TOKEN_TILES)
+                norm_and_rotate(w, a)
+        store_v()

@@ -30,6 +30,7 @@ NORMED = 2
 SLABS = 3 * PASSES
 RUN = 4
 SCALAR_COLS = 640
+FIRST_PIECES = 4
 
 FLOPS = 2 * TOKENS * D_MODEL * 3 * INNER
 
@@ -49,12 +50,18 @@ def tile_flux2parallelselfattention_pa_kernel(
         work = ctx.enter_context(tc.tile_pool(name="work", bufs=2))
         psum = ctx.enter_context(tc.psum_pool(name="psum", bufs=8))
 
-        raw = [keep.tile([P, PACK, INNER], BF16, name="raw%d" % j) for j in range(SLABS)]
+        pieces_of = [FIRST_PIECES if j == 0 else 1 for j in range(SLABS)]
+        raw = [
+            [keep.tile([P, PACK, INNER // pieces_of[j]], BF16, name="raw%d_%d" % (j, q)) for q in range(pieces_of[j])]
+            for j in range(SLABS)
+        ]
 
         def load_slab(j):
             w, c = divmod(j, PASSES)
-            rows = weights[w][c * K_PASS : (c + 1) * K_PASS, :]
-            nc.sync.dma_start(out=raw[j][:], in_=rows.rearrange("(p t) n -> p t n", t=PACK))
+            rows = weights[w][c * K_PASS : (c + 1) * K_PASS, :].rearrange("(p t) n -> p t n", t=PACK)
+            width = INNER // pieces_of[j]
+            for q in range(pieces_of[j]):
+                nc.sync.dma_start(out=raw[j][q][:], in_=rows[:, :, q * width : (q + 1) * width])
 
         x_sb = keep.tile([P, TOKEN_TILES * D_MODEL], BF16)
         cos_sb = keep.tile([P, TOKEN_TILES, HALF], BF16)
@@ -87,11 +94,13 @@ def tile_flux2parallelselfattention_pa_kernel(
 
         def regroup(j):
             grouped = stage.tile([P, INNER, PACK], BF16, align_bytes=64)
-            dst = grouped[:].rearrange("p (g i) t -> p g t i", i=RUN)
-            src = raw[j][:].rearrange("p t (g i) -> p g t i", i=RUN)
-            split = SCALAR_COLS // RUN
-            nc.scalar.copy(out=dst[:, :split], in_=src[:, :split])
-            nc.vector.tensor_copy(out=dst[:, split:], in_=src[:, split:])
+            width = INNER // pieces_of[j]
+            for q in range(pieces_of[j]):
+                dst = grouped[:, q * width : (q + 1) * width, :].rearrange("p (g i) t -> p g t i", i=RUN)
+                src = raw[j][q][:].rearrange("p t (g i) -> p g t i", i=RUN)
+                split = SCALAR_COLS // pieces_of[j] // RUN
+                nc.scalar.copy(out=dst[:, :split], in_=src[:, :split])
+                nc.vector.tensor_copy(out=dst[:, split:], in_=src[:, split:])
             grouped_of[j] = grouped
 
         def quantise(j):

@@ -28,7 +28,7 @@ HEADS_PER_BANK = BANK // HEAD
 HEADS = INNER // HEAD
 NORMED = 2
 SLABS = 3 * PASSES
-RUN = 4
+RUN = 8
 SCALAR_COLS = 640
 FIRST_PIECES = 4
 

@@ -29,8 +29,8 @@ HEADS = INNER // HEAD
 NORMED = 2
 SLABS = 3 * PASSES
 RUN = 8
-SCALAR_COLS = 640
-FIRST_PIECES = 4
+SCALAR_COLS = 576
+PIECES = [4, 2, 1, 1, 1, 1]
 
 FLOPS = 2 * TOKENS * D_MODEL * 3 * INNER
 
@@ -49,70 +49,69 @@ def tile_flux2parallelselfattention_pa_kernel(
         stage = ctx.enter_context(tc.tile_pool(name="stage", bufs=3))
         work = ctx.enter_context(tc.tile_pool(name="work", bufs=2))
         psum = ctx.enter_context(tc.psum_pool(name="psum", bufs=8))
+        ctx.enter_context(tc.manual_schedule())
 
-        pieces_of = [FIRST_PIECES if j == 0 else 1 for j in range(SLABS)]
         raw = [
-            [keep.tile([P, PACK, INNER // pieces_of[j]], BF16, name="raw%d_%d" % (j, q)) for q in range(pieces_of[j])]
+            [keep.tile([P, PACK, INNER // PIECES[j]], BF16, name="raw%d_%d" % (j, q)) for q in range(PIECES[j])]
             for j in range(SLABS)
         ]
 
         def load_slab(j):
             w, c = divmod(j, PASSES)
             rows = weights[w][c * K_PASS : (c + 1) * K_PASS, :].rearrange("(p t) n -> p t n", t=PACK)
-            width = INNER // pieces_of[j]
-            for q in range(pieces_of[j]):
+            width = INNER // PIECES[j]
+            for q in range(PIECES[j]):
                 nc.sync.dma_start(out=raw[j][q][:], in_=rows[:, :, q * width : (q + 1) * width])
 
-        x_sb = keep.tile([P, TOKEN_TILES * D_MODEL], BF16)
+        x_sb = [keep.tile([P, D_MODEL], BF16, name="x%d" % a) for a in range(TOKEN_TILES)]
         cos_sb = keep.tile([P, TOKEN_TILES, HALF], BF16)
         sin_sb = keep.tile([P, TOKEN_TILES, HALF], BF16)
-        gain_sb = keep.tile([P, NORMED, HEAD], BF16)
-
-        load_slab(0)
-        nc.sync.dma_start(
-            out=x_sb[:].rearrange("p (a k) -> p a k", a=TOKEN_TILES),
-            in_=x_rows.rearrange("(a p) k -> p a k", p=P),
-        )
-        load_slab(1)
-        nc.sync.dma_start(out=cos_sb[:], in_=cos.rearrange("(a p) i -> p a i", p=P))
-        nc.sync.dma_start(out=sin_sb[:], in_=sin.rearrange("(a p) i -> p a i", p=P))
-        for w in range(NORMED):
-            nc.sync.dma_start(out=gain_sb[:, w, :], in_=gains[w].partition_broadcast(P))
-        for j in range(2, SLABS):
-            load_slab(j)
+        gain_rows = keep.tile([P, NORMED * HEAD], BF16)
+        ones = keep.tile([P, P], BF16)
 
         ident = keep.tile([P, P], F32)
         make_identity(nc, ident[:])
         eps_sb = keep.tile([P, 1], F32)
         nc.vector.memset(eps_sb[:], EPS)
+        nc.vector.memset(gain_rows[:], 0.0)
+        nc.vector.memset(ones[:], 1.0)
+        for w in range(NORMED):
+            nc.scalar.dma_start(out=gain_rows[0:1, w * HEAD : (w + 1) * HEAD], in_=gains[w].unsqueeze(0))
         warm = keep.tile([P, 1], F32)
         nc.scalar.activation(out=warm[:], in_=eps_sb[:], func=ACT.Sqrt)
 
-        w_codes = keep.tile([P, SLABS, INNER], U32, align_bytes=64)
-        w_scales = keep.tile([P, SLABS, INNER], U8, align_bytes=64)
+        nc.sync.dma_start(out=cos_sb[:], in_=cos.rearrange("(a p) i -> p a i", p=P))
+        nc.sync.dma_start(out=sin_sb[:], in_=sin.rearrange("(a p) i -> p a i", p=P))
+        for a in range(TOKEN_TILES):
+            nc.sync.dma_start(out=x_sb[a][:], in_=x_rows[a * P : (a + 1) * P, :])
+        for j in range(SLABS):
+            load_slab(j)
+
+        w_codes = [keep.tile([P, INNER], U32, name="codes%d" % j, align_bytes=64) for j in range(SLABS)]
+        w_scales = [keep.tile([P, INNER], U8, name="scales%d" % j, align_bytes=64) for j in range(SLABS)]
         grouped_of = {}
 
-        def regroup(j):
-            grouped = stage.tile([P, INNER, PACK], BF16, align_bytes=64)
-            width = INNER // pieces_of[j]
-            for q in range(pieces_of[j]):
-                dst = grouped[:, q * width : (q + 1) * width, :].rearrange("p (g i) t -> p g t i", i=RUN)
+        def regroup(engine, j):
+            if j not in grouped_of:
+                grouped = stage.tile([P, INNER, PACK], BF16, align_bytes=64)
+                grouped_of[j] = grouped
+            width = INNER // PIECES[j]
+            split = SCALAR_COLS // PIECES[j] // RUN
+            for q in range(PIECES[j]):
+                dst = grouped_of[j][:, q * width : (q + 1) * width, :].rearrange("p (g i) t -> p g t i", i=RUN)
                 src = raw[j][q][:].rearrange("p t (g i) -> p g t i", i=RUN)
-                split = SCALAR_COLS // pieces_of[j] // RUN
-                nc.scalar.copy(out=dst[:, :split], in_=src[:, :split])
-                nc.vector.tensor_copy(out=dst[:, split:], in_=src[:, split:])
-            grouped_of[j] = grouped
+                if engine == "scalar":
+                    nc.scalar.copy(out=dst[:, :split], in_=src[:, :split])
+                else:
+                    nc.vector.tensor_copy(out=dst[:, split:], in_=src[:, split:])
 
         def quantise(j):
             nc.vector.quantize_mx(
-                out=w_codes[:, j, :].bitcast(FP8X4),
-                scales=w_scales[:, j, :],
+                out=w_codes[j][:].bitcast(FP8X4),
+                scales=w_scales[j][:],
                 in_=grouped_of[j][:].rearrange("p n t -> p (n t)"),
             )
 
-        x_words = x_sb[:].bitcast(F32).rearrange(
-            "s (a c q u) -> s a c u q", a=TOKEN_TILES, c=PASSES, q=P, u=2
-        )
         x_grouped = keep.tile([P, PASSES * TOKENS * PACK], BF16, align_bytes=64)
         x_grouped_words = x_grouped[:].bitcast(F32).rearrange(
             "p (c a s u) -> p c a s u", c=PASSES, a=TOKEN_TILES, s=P, u=2
@@ -120,17 +119,15 @@ def tile_flux2parallelselfattention_pa_kernel(
         x_codes = keep.tile([P, PASSES * TOKENS], U32, align_bytes=64)
         x_scales = keep.tile([P, PASSES * TOKENS], U8, align_bytes=64)
 
-        def transpose_x():
-            for a in range(TOKEN_TILES):
-                x_t = psum.tile([P, PASSES, 2, P], F32, tag="bank")
-                for c in range(PASSES):
-                    for u in range(2):
-                        nc.tensor.transpose(
-                            out=x_t[:, c, u, :], in_=x_words[:, a, c, u, :], identity=ident[:]
-                        )
-                nc.vector.tensor_copy(
-                    out=x_grouped_words[:, :, a, :, :], in_=x_t[:].rearrange("p c u s -> p c s u")
-                )
+        def transpose_x(a):
+            x_words = x_sb[a][:].bitcast(F32).rearrange("s (c q u) -> s c u q", c=PASSES, q=P, u=2)
+            x_t = psum.tile([P, PASSES, 2, P], F32, tag="bank")
+            for c in range(PASSES):
+                for u in range(2):
+                    nc.tensor.transpose(out=x_t[:, c, u, :], in_=x_words[:, c, u, :], identity=ident[:])
+            nc.scalar.copy(
+                out=x_grouped_words[:, :, a, :, :], in_=x_t[:].rearrange("p c u s -> p c s u")
+            )
 
         def quantise_x():
             nc.vector.quantize_mx(
@@ -151,118 +148,160 @@ def tile_flux2parallelselfattention_pa_kernel(
                         out=acc_of[(w, a, b)][:],
                         lhsT=x_codes[:, x_cols].bitcast(FP8X4),
                         lhsT_scale=x_scales[:, x_cols],
-                        rhs=w_codes[:, j, n_cols].bitcast(FP8X4),
-                        rhs_scale=w_scales[:, j, n_cols],
+                        rhs=w_codes[j][:, n_cols].bitcast(FP8X4),
+                        rhs_scale=w_scales[j][:, n_cols],
                         start=(c == 0),
                         stop=(c == PASSES - 1),
                     )
 
-        cos_gain = [keep.tile([P, TOKEN_TILES, HALF, 2], F32, name="cos_gain%d" % w) for w in range(NORMED)]
-        sin_gain = [keep.tile([P, TOKEN_TILES, 2, HALF], F32, name="sin_gain%d" % w) for w in range(NORMED)]
+        table = [keep.tile([P, TOKEN_TILES, 2, HALF, 2], F32, name="table%d" % w) for w in range(NORMED)]
+        signed_sin = keep.tile([P, TOKEN_TILES, HALF, 2], BF16)
+        gain_ps = psum.tile([P, NORMED, HEAD], F32, tag="bank")
 
-        def build_tables():
-            neg_sin = keep.tile([P, TOKEN_TILES, HALF], BF16)
-            nc.vector.tensor_scalar_mul(out=neg_sin[:], in0=sin_sb[:], scalar1=-1.0)
-            for w in range(NORMED):
-                gain_pairs = gain_sb[:, w, :].rearrange("p (i e) -> p i e", e=2)
+        def spread_gains():
+            nc.tensor.matmul(
+                out=gain_ps[:].rearrange("p w d -> p (w d)"), lhsT=ones[:], rhs=gain_rows[:], start=True, stop=True
+            )
+
+        def sign_sin():
+            nc.vector.tensor_copy(out=signed_sin[:, :, :, 0], in_=sin_sb[:])
+            nc.vector.tensor_scalar_mul(out=signed_sin[:, :, :, 1], in0=sin_sb[:], scalar1=-1.0)
+
+        def build_tables(w):
+            gain_pairs = gain_ps[:, w, :].rearrange("p (i e) -> p i e", e=2)
+            full = [P, TOKEN_TILES, HALF, 2]
+            for x, factor in enumerate((cos_sb[:].unsqueeze(3).to_broadcast(full), signed_sin[:])):
                 nc.vector.tensor_tensor(
-                    out=cos_gain[w][:],
-                    in0=cos_sb[:].unsqueeze(3).to_broadcast([P, TOKEN_TILES, HALF, 2]),
-                    in1=gain_pairs.unsqueeze(1).to_broadcast([P, TOKEN_TILES, HALF, 2]),
-                    op=ALU.mult,
-                )
-                nc.vector.tensor_tensor(
-                    out=sin_gain[w][:, :, 0, :],
-                    in0=neg_sin[:],
-                    in1=gain_pairs[:, :, 1].unsqueeze(1).to_broadcast([P, TOKEN_TILES, HALF]),
-                    op=ALU.mult,
-                )
-                nc.vector.tensor_tensor(
-                    out=sin_gain[w][:, :, 1, :],
-                    in0=sin_sb[:],
-                    in1=gain_pairs[:, :, 0].unsqueeze(1).to_broadcast([P, TOKEN_TILES, HALF]),
+                    out=table[w][:, :, x, :, :],
+                    in0=factor,
+                    in1=gain_pairs.unsqueeze(1).to_broadcast(full),
                     op=ALU.mult,
                 )
 
-        def norm_and_rotate(w, a):
+        state = {}
+
+        def open_tile(w, a):
             squares = work.tile([P, INNER], F32)
             sum_sq = work.tile([P, HEADS], F32)
-            for b in range(BANKS):
-                for h in range(HEADS_PER_BANK):
-                    head = b * HEADS_PER_BANK + h
-                    nc.scalar.activation(
-                        out=squares[:, head * HEAD : (head + 1) * HEAD],
-                        in_=acc_of[(w, a, b)][:, h * HEAD : (h + 1) * HEAD],
-                        func=ACT.Square,
-                        accum_out=sum_sq[:, head : head + 1],
-                    )
             rms = work.tile([P, HEADS], F32)
+            inv_rms = work.tile([P, HEADS], F32)
+            terms = work.tile([P, BANKS, 2, BANK], F32)
+            rotated = work.tile([P, INNER], F32)
+            state[(w, a)] = (squares, sum_sq, rms, inv_rms, terms, rotated)
+
+        def rotary_products(w, a, b):
+            terms = state[(w, a)][4]
+            shape = [P, 2, HEADS_PER_BANK, HEAD]
+            nc.vector.tensor_tensor(
+                out=terms[:, b, :, :].rearrange("p x (h d) -> p x h d", h=HEADS_PER_BANK),
+                in0=acc_of[(w, a, b)][:].rearrange("p (h d) -> p h d", h=HEADS_PER_BANK).unsqueeze(1).to_broadcast(shape),
+                in1=table[w][:, a, :, :, :].rearrange("p x i e -> p x (i e)").unsqueeze(2).to_broadcast(shape),
+                op=ALU.mult,
+            )
+
+        def sums_of_squares(w, a, b):
+            squares, sum_sq = state[(w, a)][0:2]
+            for h in range(HEADS_PER_BANK):
+                head = b * HEADS_PER_BANK + h
+                nc.scalar.activation(
+                    out=squares[:, head * HEAD : (head + 1) * HEAD],
+                    in_=acc_of[(w, a, b)][:, h * HEAD : (h + 1) * HEAD],
+                    func=ACT.Square,
+                    accum_out=sum_sq[:, head : head + 1],
+                )
+
+        def root(w, a):
+            sum_sq, rms = state[(w, a)][1:3]
             nc.scalar.activation(
                 out=rms[:], in_=sum_sq[:], func=ACT.Sqrt, bias=eps_sb[:, 0:1], scale=1.0 / HEAD
             )
 
-            direct = work.tile([P, INNER], F32)
-            cross = work.tile([P, BANKS, 2, BANK // 2], F32)
-            for b in range(BANKS):
-                acc = acc_of[(w, a, b)]
-                acc_pairs = acc[:].rearrange("p (n e) -> p e n", e=2)
-                for e in range(2):
-                    nc.vector.tensor_tensor(
-                        out=cross[:, b, e, :].rearrange("p (h i) -> p h i", h=HEADS_PER_BANK),
-                        in0=acc_pairs[:, 1 - e, :].rearrange("p (h i) -> p h i", h=HEADS_PER_BANK),
-                        in1=sin_gain[w][:, a, e, :].unsqueeze(1).to_broadcast([P, HEADS_PER_BANK, HALF]),
-                        op=ALU.mult,
-                    )
-                nc.vector.tensor_tensor(
-                    out=direct[:, b * BANK : (b + 1) * BANK].rearrange("p (h d) -> p h d", h=HEADS_PER_BANK),
-                    in0=acc[:].rearrange("p (h d) -> p h d", h=HEADS_PER_BANK),
-                    in1=cos_gain[w][:, a, :, :]
-                    .rearrange("p i e -> p (i e)")
-                    .unsqueeze(1)
-                    .to_broadcast([P, HEADS_PER_BANK, HEAD]),
-                    op=ALU.mult,
-                )
-            direct_pairs = direct[:].rearrange("p (b n e) -> p b n e", b=BANKS, e=2)
-            nc.vector.tensor_tensor(
-                out=direct_pairs, in0=direct_pairs, in1=cross[:].rearrange("p b e n -> p b n e"), op=ALU.add
-            )
-            inv_rms = work.tile([P, HEADS], F32)
+        def invert(w, a):
+            rms, inv_rms = state[(w, a)][2:4]
             nc.vector.reciprocal(out=inv_rms[:], in_=rms[:])
 
-            rotated = work.tile([P, INNER], F32)
-            for head in range(HEADS):
-                cols = slice(head * HEAD, (head + 1) * HEAD)
+        def add_products(w, a, banks):
+            terms = state[(w, a)][4]
+            first = terms[:, banks, 0, :].rearrange("p b (n e) -> p b n e", e=2)
+            second = terms[:, banks, 1, :].rearrange("p b (n e) -> p b n e", e=2)
+            nc.vector.tensor_tensor(out=first, in0=first, in1=second[:, :, :, ::-1], op=ALU.add)
+
+        def scale_and_store(w, a, b):
+            inv_rms, terms, rotated = state[(w, a)][3:6]
+            for h in range(HEADS_PER_BANK):
+                head = b * HEADS_PER_BANK + h
                 nc.scalar.activation(
-                    out=rotated[:, cols], in_=direct[:, cols], func=ACT.Copy, scale=inv_rms[:, head : head + 1]
+                    out=rotated[:, head * HEAD : (head + 1) * HEAD],
+                    in_=terms[:, b, 0, h * HEAD : (h + 1) * HEAD],
+                    func=ACT.Copy,
+                    scale=inv_rms[:, head : head + 1],
                 )
-            nc.sync.dma_start(out=outs[w][a * P : (a + 1) * P, :], in_=rotated[:])
+            cols = slice(b * BANK, (b + 1) * BANK)
+            nc.sync.dma_start(out=outs[w][a * P : (a + 1) * P, cols], in_=rotated[:, cols])
 
-        def store_v():
-            w = NORMED
-            for a in range(TOKEN_TILES):
-                for b in range(BANKS):
-                    plain = work.tile([P, BANK], F32, bufs=TOKEN_TILES * BANKS)
-                    if b % 2 == 0:
-                        nc.scalar.copy(out=plain[:], in_=acc_of[(w, a, b)][:])
-                    else:
-                        nc.vector.tensor_copy(out=plain[:], in_=acc_of[(w, a, b)][:])
-                    nc.sync.dma_start(
-                        out=outs[w][a * P : (a + 1) * P, b * BANK : (b + 1) * BANK], in_=plain[:]
-                    )
+        def store_v(engine, a, b):
+            plain = work.tile([P, BANK], F32, bufs=TOKEN_TILES * BANKS)
+            if engine == "scalar":
+                nc.scalar.copy(out=plain[:], in_=acc_of[(NORMED, a, b)][:])
+            else:
+                nc.vector.tensor_copy(out=plain[:], in_=acc_of[(NORMED, a, b)][:])
+            nc.sync.dma_start(
+                out=outs[NORMED][a * P : (a + 1) * P, b * BANK : (b + 1) * BANK], in_=plain[:]
+            )
 
-        regroup(0)
-        transpose_x()
-        regroup(1)
+        def both(j):
+            regroup("scalar", j)
+            regroup("vector", j)
+
+        spread_gains()
+        sign_sin()
+        for a in range(TOKEN_TILES):
+            transpose_x(a)
+        build_tables(0)
+        both(0)
         quantise_x()
+        both(1)
         quantise(0)
         multiply(0)
-        build_tables()
-        for j in range(1, SLABS):
-            if j + 1 < SLABS:
-                regroup(j + 1)
+        build_tables(1)
+        quantise(1)
+        multiply(1)
+        both(2)
+        tiles = [(w, a) for w in range(NORMED) for a in range(TOKEN_TILES)]
+        every_bank = slice(0, BANKS)
+        for n, (w, a) in enumerate(tiles[:-1]):
+            j = PASSES + n
+            open_tile(w, a)
+            rotary_products(w, a, 0)
+            sums_of_squares(w, a, 1)
+            rotary_products(w, a, 1)
+            sums_of_squares(w, a, 0)
+            root(w, a)
+            if n > 0:
+                for b in range(BANKS):
+                    scale_and_store(*tiles[n - 1], b)
+            both(j + 1)
             quantise(j)
             multiply(j)
-            if j >= PASSES:
-                w, a = divmod(j - PASSES, TOKEN_TILES)
-                norm_and_rotate(w, a)
-        store_v()
+            invert(w, a)
+            add_products(w, a, every_bank)
+        w, a = tiles[-1]
+        open_tile(w, a)
+        quantise(SLABS - 1)
+        multiply(SLABS - 1)
+        sums_of_squares(w, a, 0)
+        sums_of_squares(w, a, 1)
+        root(w, a)
+        rotary_products(w, a, 0)
+        for b in range(BANKS):
+            scale_and_store(*tiles[-2], b)
+        store_v("scalar", 0, 0)
+        store_v("scalar", 0, 1)
+        store_v("scalar", 1, 0)
+        invert(w, a)
+        store_v("vector", 1, 1)
+        add_products(w, a, slice(0, 1))
+        rotary_products(w, a, 1)
+        scale_and_store(w, a, 0)
+        add_products(w, a, slice(1, 2))
+        scale_and_store(w, a, 1)

@@ -29,8 +29,8 @@ HEADS = INNER // HEAD
 NORMED = 2
 SLABS = 3 * PASSES
 RUN = 8
-SCALAR_COLS = 576
-PIECES = [4, 2, 1, 1, 1, 1]
+SCALAR_COLS = [512, 512, 640, 896, 896, 896]
+PIECES = [4, 2, 2, 1, 1, 1]
 
 FLOPS = 2 * TOKENS * D_MODEL * 3 * INNER
 
@@ -66,17 +66,16 @@ def tile_flux2parallelselfattention_pa_kernel(
         x_sb = [keep.tile([P, D_MODEL], BF16, name="x%d" % a) for a in range(TOKEN_TILES)]
         cos_sb = keep.tile([P, TOKEN_TILES, HALF], BF16)
         sin_sb = keep.tile([P, TOKEN_TILES, HALF], BF16)
-        gain_rows = keep.tile([P, NORMED * HEAD], BF16)
-        ones = keep.tile([P, P], BF16)
+        gain_cols = [keep.tile([P, 1], BF16, name="gain%d" % w) for w in range(NORMED)]
 
         ident = keep.tile([P, P], F32)
         make_identity(nc, ident[:])
         eps_sb = keep.tile([P, 1], F32)
         nc.vector.memset(eps_sb[:], EPS)
-        nc.vector.memset(gain_rows[:], 0.0)
-        nc.vector.memset(ones[:], 1.0)
+        ident_bf = keep.tile([P, P], BF16)
+        make_identity(nc, ident_bf[:])
         for w in range(NORMED):
-            nc.scalar.dma_start(out=gain_rows[0:1, w * HEAD : (w + 1) * HEAD], in_=gains[w].unsqueeze(0))
+            nc.scalar.dma_start(out=gain_cols[w][:], in_=gains[w].unsqueeze(1))
         warm = keep.tile([P, 1], F32)
         nc.scalar.activation(out=warm[:], in_=eps_sb[:], func=ACT.Sqrt)
 
@@ -96,7 +95,7 @@ def tile_flux2parallelselfattention_pa_kernel(
                 grouped = stage.tile([P, INNER, PACK], BF16, align_bytes=64)
                 grouped_of[j] = grouped
             width = INNER // PIECES[j]
-            split = SCALAR_COLS // PIECES[j] // RUN
+            split = SCALAR_COLS[j] // PIECES[j] // RUN
             for q in range(PIECES[j]):
                 dst = grouped_of[j][:, q * width : (q + 1) * width, :].rearrange("p (g i) t -> p g t i", i=RUN)
                 src = raw[j][q][:].rearrange("p t (g i) -> p g t i", i=RUN)
@@ -159,9 +158,14 @@ def tile_flux2parallelselfattention_pa_kernel(
         gain_ps = psum.tile([P, NORMED, HEAD], F32, tag="bank")
 
         def spread_gains():
-            nc.tensor.matmul(
-                out=gain_ps[:].rearrange("p w d -> p (w d)"), lhsT=ones[:], rhs=gain_rows[:], start=True, stop=True
-            )
+            for w in range(NORMED):
+                nc.tensor.matmul(
+                    out=gain_ps[:, w, :],
+                    lhsT=gain_cols[w][:].to_broadcast([P, P]),
+                    rhs=ident_bf[:],
+                    start=True,
+                    stop=True,
+                )
 
         def sign_sin():
             nc.vector.tensor_copy(out=signed_sin[:, :, :, 0], in_=sin_sb[:])
@@ -185,19 +189,23 @@ def tile_flux2parallelselfattention_pa_kernel(
             sum_sq = work.tile([P, HEADS], F32)
             rms = work.tile([P, HEADS], F32)
             inv_rms = work.tile([P, HEADS], F32)
-            terms = work.tile([P, BANKS, 2, BANK], F32)
+            terms = work.tile([P, HEADS, 2, HEAD], F32)
             rotated = work.tile([P, INNER], F32)
             state[(w, a)] = (squares, sum_sq, rms, inv_rms, terms, rotated)
 
         def rotary_products(w, a, b):
-            terms = state[(w, a)][4]
-            shape = [P, 2, HEADS_PER_BANK, HEAD]
-            nc.vector.tensor_tensor(
-                out=terms[:, b, :, :].rearrange("p x (h d) -> p x h d", h=HEADS_PER_BANK),
-                in0=acc_of[(w, a, b)][:].rearrange("p (h d) -> p h d", h=HEADS_PER_BANK).unsqueeze(1).to_broadcast(shape),
-                in1=table[w][:, a, :, :, :].rearrange("p x i e -> p x (i e)").unsqueeze(2).to_broadcast(shape),
-                op=ALU.mult,
-            )
+            inv_rms, terms = state[(w, a)][3:5]
+            shape = [P, 2, HEAD]
+            for h in range(HEADS_PER_BANK):
+                head = b * HEADS_PER_BANK + h
+                nc.vector.scalar_tensor_tensor(
+                    out=terms[:, head, :, :],
+                    in0=acc_of[(w, a, b)][:, h * HEAD : (h + 1) * HEAD].unsqueeze(1).to_broadcast(shape),
+                    scalar=inv_rms[:, head : head + 1],
+                    in1=table[w][:, a, :, :, :].rearrange("p x i e -> p x (i e)"),
+                    op0=ALU.mult,
+                    op1=ALU.mult,
+                )
 
         def sums_of_squares(w, a, b):
             squares, sum_sq = state[(w, a)][0:2]
@@ -220,23 +228,18 @@ def tile_flux2parallelselfattention_pa_kernel(
             rms, inv_rms = state[(w, a)][2:4]
             nc.vector.reciprocal(out=inv_rms[:], in_=rms[:])
 
-        def add_products(w, a, banks):
-            terms = state[(w, a)][4]
-            first = terms[:, banks, 0, :].rearrange("p b (n e) -> p b n e", e=2)
-            second = terms[:, banks, 1, :].rearrange("p b (n e) -> p b n e", e=2)
-            nc.vector.tensor_tensor(out=first, in0=first, in1=second[:, :, :, ::-1], op=ALU.add)
-
-        def scale_and_store(w, a, b):
-            inv_rms, terms, rotated = state[(w, a)][3:6]
-            for h in range(HEADS_PER_BANK):
-                head = b * HEADS_PER_BANK + h
-                nc.scalar.activation(
-                    out=rotated[:, head * HEAD : (head + 1) * HEAD],
-                    in_=terms[:, b, 0, h * HEAD : (h + 1) * HEAD],
-                    func=ACT.Copy,
-                    scale=inv_rms[:, head : head + 1],
-                )
-            cols = slice(b * BANK, (b + 1) * BANK)
+        def add_and_store(w, a, banks):
+            terms, rotated = state[(w, a)][4:6]
+            heads = slice(banks.start * HEADS_PER_BANK, banks.stop * HEADS_PER_BANK)
+            cols = slice(banks.start * BANK, banks.stop * BANK)
+            first = terms[:, heads, 0, :].rearrange("p h (i e) -> p h i e", e=2)
+            second = terms[:, heads, 1, :].rearrange("p h (i e) -> p h i e", e=2)
+            nc.vector.tensor_tensor(
+                out=rotated[:, cols].rearrange("p (h i e) -> p h i e", i=HALF, e=2),
+                in0=first,
+                in1=second[:, :, :, ::-1],
+                op=ALU.add,
+            )
             nc.sync.dma_start(out=outs[w][a * P : (a + 1) * P, cols], in_=rotated[:, cols])
 
         def store_v(engine, a, b):
@@ -253,8 +256,16 @@ def tile_flux2parallelselfattention_pa_kernel(
             regroup("scalar", j)
             regroup("vector", j)
 
-        spread_gains()
+        tiles = [(w, a) for w in range(NORMED) for a in range(TOKEN_TILES)]
+
+        def norm(w, a):
+            open_tile(w, a)
+            for b in range(BANKS):
+                sums_of_squares(w, a, b)
+            root(w, a)
+
         sign_sin()
+        spread_gains()
         for a in range(TOKEN_TILES):
             transpose_x(a)
         build_tables(0)
@@ -267,41 +278,21 @@ def tile_flux2parallelselfattention_pa_kernel(
         quantise(1)
         multiply(1)
         both(2)
-        tiles = [(w, a) for w in range(NORMED) for a in range(TOKEN_TILES)]
-        every_bank = slice(0, BANKS)
-        for n, (w, a) in enumerate(tiles[:-1]):
+        for n, (w, a) in enumerate(tiles):
             j = PASSES + n
-            open_tile(w, a)
-            rotary_products(w, a, 0)
-            sums_of_squares(w, a, 1)
-            rotary_products(w, a, 1)
-            sums_of_squares(w, a, 0)
-            root(w, a)
-            if n > 0:
-                for b in range(BANKS):
-                    scale_and_store(*tiles[n - 1], b)
-            both(j + 1)
+            norm(w, a)
             quantise(j)
             multiply(j)
+            if j + 1 < SLABS:
+                both(j + 1)
             invert(w, a)
-            add_products(w, a, every_bank)
-        w, a = tiles[-1]
-        open_tile(w, a)
-        quantise(SLABS - 1)
-        multiply(SLABS - 1)
-        sums_of_squares(w, a, 0)
-        sums_of_squares(w, a, 1)
-        root(w, a)
-        rotary_products(w, a, 0)
-        for b in range(BANKS):
-            scale_and_store(*tiles[-2], b)
-        store_v("scalar", 0, 0)
-        store_v("scalar", 0, 1)
-        store_v("scalar", 1, 0)
-        invert(w, a)
-        store_v("vector", 1, 1)
-        add_products(w, a, slice(0, 1))
-        rotary_products(w, a, 1)
-        scale_and_store(w, a, 0)
-        add_products(w, a, slice(1, 2))
-        scale_and_store(w, a, 1)
+            last = n == len(tiles) - 1
+            if last:
+                for b in range(TOKEN_TILES * BANKS):
+                    store_v("scalar", *divmod(b, BANKS))
+            for b in range(BANKS):
+                rotary_products(w, a, b)
+                if last:
+                    add_and_store(w, a, slice(b, b + 1))
+            if not last:
+                add_and_store(w, a, slice(0, BANKS))

@@ -29,7 +29,7 @@ HEADS = INNER // HEAD
 NORMED = 2
 SLABS = 3 * PASSES
 RUN = 8
-SCALAR_COLS = [512, 512, 640, 896, 896, 896]
+SCALAR_COLS = [448, 448, 640, 832, 832, 832]
 PIECES = [4, 2, 2, 1, 1, 1]
 
 FLOPS = 2 * TOKENS * D_MODEL * 3 * INNER

@@ -29,7 +29,7 @@ HEADS = INNER // HEAD
 NORMED = 2
 SLABS = 3 * PASSES
 RUN = 8
-SCALAR_COLS = [448, 448, 640, 832, 832, 832]
+SCALAR_COLS = [512, 512, 512, 128, 896, 704]
 PIECES = [4, 2, 2, 1, 1, 1]
 
 FLOPS = 2 * TOKENS * D_MODEL * 3 * INNER
@@ -228,13 +228,13 @@ def tile_flux2parallelselfattention_pa_kernel(
             rms, inv_rms = state[(w, a)][2:4]
             nc.vector.reciprocal(out=inv_rms[:], in_=rms[:])
 
-        def add_and_store(w, a, banks):
+        def add_and_store(engine, w, a, banks):
             terms, rotated = state[(w, a)][4:6]
             heads = slice(banks.start * HEADS_PER_BANK, banks.stop * HEADS_PER_BANK)
             cols = slice(banks.start * BANK, banks.stop * BANK)
             first = terms[:, heads, 0, :].rearrange("p h (i e) -> p h i e", e=2)
             second = terms[:, heads, 1, :].rearrange("p h (i e) -> p h i e", e=2)
-            nc.vector.tensor_tensor(
+            engine.tensor_tensor(
                 out=rotated[:, cols].rearrange("p (h i e) -> p h i e", i=HALF, e=2),
                 in0=first,
                 in1=second[:, :, :, ::-1],
@@ -258,41 +258,55 @@ def tile_flux2parallelselfattention_pa_kernel(
 
         tiles = [(w, a) for w in range(NORMED) for a in range(TOKEN_TILES)]
 
+        def rotate_pair(w):
+            invert(w, 0)
+            rotary_products(w, 0, 0)
+            invert(w, 1)
+            rotary_products(w, 0, 1)
+            for b in range(BANKS):
+                rotary_products(w, 1, b)
+            add_and_store(nc.gpsimd, w, 0, whole)
+
         def norm(w, a):
             open_tile(w, a)
             for b in range(BANKS):
                 sums_of_squares(w, a, b)
             root(w, a)
 
+        whole = slice(0, BANKS)
         sign_sin()
         spread_gains()
         for a in range(TOKEN_TILES):
             transpose_x(a)
-        build_tables(0)
+        for w in range(NORMED):
+            build_tables(w)
         both(0)
         quantise_x()
         both(1)
         quantise(0)
         multiply(0)
-        build_tables(1)
+        both(2)
         quantise(1)
         multiply(1)
-        both(2)
-        for n, (w, a) in enumerate(tiles):
-            j = PASSES + n
-            norm(w, a)
-            quantise(j)
-            multiply(j)
-            if j + 1 < SLABS:
-                both(j + 1)
-            invert(w, a)
-            last = n == len(tiles) - 1
-            if last:
-                for b in range(TOKEN_TILES * BANKS):
-                    store_v("scalar", *divmod(b, BANKS))
-            for b in range(BANKS):
-                rotary_products(w, a, b)
-                if last:
-                    add_and_store(w, a, slice(b, b + 1))
-            if not last:
-                add_and_store(w, a, slice(0, BANKS))
+        for a in range(TOKEN_TILES):
+            norm(0, a)
+        both(3)
+        quantise(2)
+        multiply(2)
+        rotate_pair(0)
+        both(4)
+        quantise(3)
+        multiply(3)
+        add_and_store(nc.vector, 0, 1, whole)
+        both(5)
+        for a in range(TOKEN_TILES):
+            norm(1, a)
+        quantise(4)
+        multiply(4)
+        quantise(5)
+        multiply(5)
+        for b in range(TOKEN_TILES * BANKS):
+            store_v("scalar", *divmod(b, BANKS))
+        rotate_pair(1)
+        for b in range(BANKS):
+            add_and_store(nc.vector, 1, 1, slice(b, b + 1))

@@ -30,7 +30,7 @@ NORMED = 2
 SLABS = 3 * PASSES
 RUN = 8
 SCALAR_COLS = [512, 512, 512, 128, 896, 704]
-PIECES = [4, 2, 2, 1, 1, 1]
+PIECES = [1, 1, 1, 1, 1, 1]
 
 FLOPS = 2 * TOKENS * D_MODEL * 3 * INNER
 
@@ -41,8 +41,8 @@ def tile_flux2parallelselfattention_pa_kernel(
     nc = tc.nc
     weights = [w_q, w_k, w_v]
     gains = [norm_q_w, norm_k_w]
-    outs = [o.rearrange("b s h d -> (b s) (h d)") for o in (out_0, out_1, out_2)]
-    x_rows = hidden_states.rearrange("b s k -> (b s) k")
+    outs = [o.rearrange("b (p a) h d -> a (b p) (h d)", a=TOKEN_TILES) for o in (out_0, out_1, out_2)]
+    x_rows = hidden_states.rearrange("b (p a) k -> (b p) (a k)", a=TOKEN_TILES)
 
     with ExitStack() as ctx:
         keep = ctx.enter_context(tc.tile_pool(name="keep", bufs=1))
@@ -63,7 +63,7 @@ def tile_flux2parallelselfattention_pa_kernel(
             for q in range(PIECES[j]):
                 nc.sync.dma_start(out=raw[j][q][:], in_=rows[:, :, q * width : (q + 1) * width])
 
-        x_sb = [keep.tile([P, D_MODEL], BF16, name="x%d" % a) for a in range(TOKEN_TILES)]
+        x_sb = keep.tile([P, TOKEN_TILES, D_MODEL], BF16)
         cos_sb = keep.tile([P, TOKEN_TILES, HALF], BF16)
         sin_sb = keep.tile([P, TOKEN_TILES, HALF], BF16)
         gain_cols = [keep.tile([P, 1], BF16, name="gain%d" % w) for w in range(NORMED)]
@@ -79,10 +79,9 @@ def tile_flux2parallelselfattention_pa_kernel(
         warm = keep.tile([P, 1], F32)
         nc.scalar.activation(out=warm[:], in_=eps_sb[:], func=ACT.Sqrt)
 
-        nc.sync.dma_start(out=cos_sb[:], in_=cos.rearrange("(a p) i -> p a i", p=P))
-        nc.sync.dma_start(out=sin_sb[:], in_=sin.rearrange("(a p) i -> p a i", p=P))
-        for a in range(TOKEN_TILES):
-            nc.sync.dma_start(out=x_sb[a][:], in_=x_rows[a * P : (a + 1) * P, :])
+        nc.sync.dma_start(out=cos_sb[:], in_=cos.rearrange("(p a) i -> p a i", p=P))
+        nc.sync.dma_start(out=sin_sb[:], in_=sin.rearrange("(p a) i -> p a i", p=P))
+        nc.sync.dma_start(out=x_sb[:].rearrange("p a k -> p (a k)"), in_=x_rows)
         for j in range(SLABS):
             load_slab(j)
 
@@ -119,7 +118,7 @@ def tile_flux2parallelselfattention_pa_kernel(
         x_scales = keep.tile([P, PASSES * TOKENS], U8, align_bytes=64)
 
         def transpose_x(a):
-            x_words = x_sb[a][:].bitcast(F32).rearrange("s (c q u) -> s c u q", c=PASSES, q=P, u=2)
+            x_words = x_sb[:, a, :].bitcast(F32).rearrange("s (c q u) -> s c u q", c=PASSES, q=P, u=2)
             x_t = psum.tile([P, PASSES, 2, P], F32, tag="bank")
             for c in range(PASSES):
                 for u in range(2):
@@ -240,7 +239,7 @@ def tile_flux2parallelselfattention_pa_kernel(
                 in1=second[:, :, :, ::-1],
                 op=ALU.add,
             )
-            nc.sync.dma_start(out=outs[w][a * P : (a + 1) * P, cols], in_=rotated[:, cols])
+            nc.sync.dma_start(out=outs[w][a][:, cols], in_=rotated[:, cols])
 
         def store_v(engine, a, b):
             plain = work.tile([P, BANK], F32, bufs=TOKEN_TILES * BANKS)
@@ -249,7 +248,7 @@ def tile_flux2parallelselfattention_pa_kernel(
             else:
                 nc.vector.tensor_copy(out=plain[:], in_=acc_of[(NORMED, a, b)][:])
             nc.sync.dma_start(
-                out=outs[NORMED][a * P : (a + 1) * P, b * BANK : (b + 1) * BANK], in_=plain[:]
+                out=outs[NORMED][a][:, b * BANK : (b + 1) * BANK], in_=plain[:]
             )
 
         def both(j):

@@ -29,8 +29,9 @@ HEADS = INNER // HEAD
 NORMED = 2
 SLABS = 3 * PASSES
 RUN = 8
-SCALAR_COLS = [512, 512, 512, 128, 896, 704]
-PIECES = [1, 1, 1, 1, 1, 1]
+PROJ = [0,1,2]
+SCALAR_COLS = [576,448,576,256,512,640]
+PARTS = [2,1,1,1,1,1]
 
 FLOPS = 2 * TOKENS * D_MODEL * 3 * INNER
 
@@ -47,21 +48,21 @@ def tile_flux2parallelselfattention_pa_kernel(
     with ExitStack() as ctx:
         keep = ctx.enter_context(tc.tile_pool(name="keep", bufs=1))
         stage = ctx.enter_context(tc.tile_pool(name="stage", bufs=3))
-        work = ctx.enter_context(tc.tile_pool(name="work", bufs=2))
-        psum = ctx.enter_context(tc.psum_pool(name="psum", bufs=8))
+        work = ctx.enter_context(tc.tile_pool(name="work", bufs=4))
+        psum = ctx.enter_context(tc.psum_pool(name="psum", bufs=1))
         ctx.enter_context(tc.manual_schedule())
 
         raw = [
-            [keep.tile([P, PACK, INNER // PIECES[j]], BF16, name="raw%d_%d" % (j, q)) for q in range(PIECES[j])]
+            [keep.tile([P, PACK // PARTS[j], INNER], BF16, name="raw%d_%d" % (j, u)) for u in range(PARTS[j])]
             for j in range(SLABS)
         ]
 
-        def load_slab(j):
-            w, c = divmod(j, PASSES)
+        def load_slab(j, parts=None):
+            w, c = PROJ[j // PASSES], j % PASSES
             rows = weights[w][c * K_PASS : (c + 1) * K_PASS, :].rearrange("(p t) n -> p t n", t=PACK)
-            width = INNER // PIECES[j]
-            for q in range(PIECES[j]):
-                nc.sync.dma_start(out=raw[j][q][:], in_=rows[:, :, q * width : (q + 1) * width])
+            depth = PACK // PARTS[j]
+            for u in range(PARTS[j]) if parts is None else parts:
+                nc.sync.dma_start(out=raw[j][u][:], in_=rows[:, u * depth : (u + 1) * depth, :])
 
         x_sb = keep.tile([P, TOKEN_TILES, D_MODEL], BF16)
         cos_sb = keep.tile([P, TOKEN_TILES, HALF], BF16)
@@ -77,37 +78,44 @@ def tile_flux2parallelselfattention_pa_kernel(
         for w in range(NORMED):
             nc.scalar.dma_start(out=gain_cols[w][:], in_=gains[w].unsqueeze(1))
         warm = keep.tile([P, 1], F32)
-        nc.scalar.activation(out=warm[:], in_=eps_sb[:], func=ACT.Sqrt)
+        nc.scalar.activation(out=warm[:], in_=eps_sb[:], func=ACT.Abs_reciprocal_sqrt)
 
+        load_slab(0, [0])
         nc.sync.dma_start(out=cos_sb[:], in_=cos.rearrange("(p a) i -> p a i", p=P))
         nc.sync.dma_start(out=sin_sb[:], in_=sin.rearrange("(p a) i -> p a i", p=P))
+        load_slab(0, [1])
         nc.sync.dma_start(out=x_sb[:].rearrange("p a k -> p (a k)"), in_=x_rows)
-        for j in range(SLABS):
+        for j in range(1, SLABS):
             load_slab(j)
 
         w_codes = [keep.tile([P, INNER], U32, name="codes%d" % j, align_bytes=64) for j in range(SLABS)]
         w_scales = [keep.tile([P, INNER], U8, name="scales%d" % j, align_bytes=64) for j in range(SLABS)]
         grouped_of = {}
 
-        def regroup(engine, j):
+        def regroup(engine, j, part=None, first=0, last=INNER):
             if j not in grouped_of:
                 grouped = stage.tile([P, INNER, PACK], BF16, align_bytes=64)
                 grouped_of[j] = grouped
-            width = INNER // PIECES[j]
-            split = SCALAR_COLS[j] // PIECES[j] // RUN
-            for q in range(PIECES[j]):
-                dst = grouped_of[j][:, q * width : (q + 1) * width, :].rearrange("p (g i) t -> p g t i", i=RUN)
-                src = raw[j][q][:].rearrange("p t (g i) -> p g t i", i=RUN)
+            split = SCALAR_COLS[j]
+            for u in range(PARTS[j]) if part is None else [part]:
                 if engine == "scalar":
-                    nc.scalar.copy(out=dst[:, :split], in_=src[:, :split])
+                    regroup_columns(nc.scalar.copy, j, u, first, min(last, split))
                 else:
-                    nc.vector.tensor_copy(out=dst[:, split:], in_=src[:, split:])
+                    regroup_columns(nc.vector.tensor_copy, j, u, max(first, split), last)
 
-        def quantise(j):
+        def regroup_columns(copy, j, u, first, last):
+            if first < last:
+                depth = PACK // PARTS[j]
+                copy(
+                    out=grouped_of[j][:, first:last, u * depth : (u + 1) * depth].rearrange("p (g i) t -> p g t i", i=RUN),
+                    in_=raw[j][u][:, :, first:last].rearrange("p t (g i) -> p g t i", i=RUN),
+                )
+
+        def quantise(j, first=0, last=INNER):
             nc.vector.quantize_mx(
-                out=w_codes[j][:].bitcast(FP8X4),
-                scales=w_scales[j][:],
-                in_=grouped_of[j][:].rearrange("p n t -> p (n t)"),
+                out=w_codes[j][:, first:last].bitcast(FP8X4),
+                scales=w_scales[j][:, first:last],
+                in_=grouped_of[j][:, first:last, :].rearrange("p n t -> p (n t)"),
             )
 
         x_grouped = keep.tile([P, PASSES * TOKENS * PACK], BF16, align_bytes=64)
@@ -119,7 +127,7 @@ def tile_flux2parallelselfattention_pa_kernel(
 
         def transpose_x(a):
             x_words = x_sb[:, a, :].bitcast(F32).rearrange("s (c q u) -> s c u q", c=PASSES, q=P, u=2)
-            x_t = psum.tile([P, PASSES, 2, P], F32, tag="bank")
+            x_t = psum.tile([P, PASSES, 2, P], F32, tag="bank%d" % (5 + a))
             for c in range(PASSES):
                 for u in range(2):
                     nc.tensor.transpose(out=x_t[:, c, u, :], in_=x_words[:, c, u, :], identity=ident[:])
@@ -134,14 +142,15 @@ def tile_flux2parallelselfattention_pa_kernel(
 
         acc_of = {}
 
-        def multiply(j):
-            w, c = divmod(j, PASSES)
-            for a in range(TOKEN_TILES):
+        def multiply(j, tokens=range(TOKEN_TILES)):
+            w, c = PROJ[j // PASSES], j % PASSES
+            for a in tokens:
                 x_cols = slice((c * TOKEN_TILES + a) * P, (c * TOKEN_TILES + a + 1) * P)
                 for b in range(BANKS):
                     n_cols = slice(b * BANK, (b + 1) * BANK)
                     if c == 0:
-                        acc_of[(w, a, b)] = psum.tile([P, BANK], F32, tag="bank", name="acc")
+                        at = (PROJ.index(w) % 2 * TOKEN_TILES + a) * BANKS + b
+                        acc_of[(w, a, b)] = psum.tile([P, BANK], F32, tag="bank%d" % at, name="acc")
                     nc.tensor.matmul_mx(
                         out=acc_of[(w, a, b)][:],
                         lhsT=x_codes[:, x_cols].bitcast(FP8X4),
@@ -154,7 +163,7 @@ def tile_flux2parallelselfattention_pa_kernel(
 
         table = [keep.tile([P, TOKEN_TILES, 2, HALF, 2], F32, name="table%d" % w) for w in range(NORMED)]
         signed_sin = keep.tile([P, TOKEN_TILES, HALF, 2], BF16)
-        gain_ps = psum.tile([P, NORMED, HEAD], F32, tag="bank")
+        gain_ps = psum.tile([P, NORMED, HEAD], F32, tag="bank4")
 
         def spread_gains():
             for w in range(NORMED):
@@ -186,14 +195,13 @@ def tile_flux2parallelselfattention_pa_kernel(
         def open_tile(w, a):
             squares = work.tile([P, INNER], F32)
             sum_sq = work.tile([P, HEADS], F32)
-            rms = work.tile([P, HEADS], F32)
             inv_rms = work.tile([P, HEADS], F32)
             terms = work.tile([P, HEADS, 2, HEAD], F32)
             rotated = work.tile([P, INNER], F32)
-            state[(w, a)] = (squares, sum_sq, rms, inv_rms, terms, rotated)
+            state[(w, a)] = (squares, sum_sq, inv_rms, terms, rotated)
 
         def rotary_products(w, a, b):
-            inv_rms, terms = state[(w, a)][3:5]
+            inv_rms, terms = state[(w, a)][2:4]
             shape = [P, 2, HEAD]
             for h in range(HEADS_PER_BANK):
                 head = b * HEADS_PER_BANK + h
@@ -218,19 +226,14 @@ def tile_flux2parallelselfattention_pa_kernel(
                 )
 
         def root(w, a):
-            sum_sq, rms = state[(w, a)][1:3]
+            sum_sq, inv_rms = state[(w, a)][1:3]
             nc.scalar.activation(
-                out=rms[:], in_=sum_sq[:], func=ACT.Sqrt, bias=eps_sb[:, 0:1], scale=1.0 / HEAD
+                out=inv_rms[:], in_=sum_sq[:], func=ACT.Abs_reciprocal_sqrt, bias=eps_sb[:, 0:1], scale=1.0 / HEAD
             )
 
-        def invert(w, a):
-            rms, inv_rms = state[(w, a)][2:4]
-            nc.vector.reciprocal(out=inv_rms[:], in_=rms[:])
-
-        def add_and_store(engine, w, a, banks):
-            terms, rotated = state[(w, a)][4:6]
-            heads = slice(banks.start * HEADS_PER_BANK, banks.stop * HEADS_PER_BANK)
-            cols = slice(banks.start * BANK, banks.stop * BANK)
+        def add_heads(engine, w, a, heads):
+            terms, rotated = state[(w, a)][3:5]
+            cols = slice(heads.start * HEAD, heads.stop * HEAD)
             first = terms[:, heads, 0, :].rearrange("p h (i e) -> p h i e", e=2)
             second = terms[:, heads, 1, :].rearrange("p h (i e) -> p h i e", e=2)
             engine.tensor_tensor(
@@ -239,73 +242,118 @@ def tile_flux2parallelselfattention_pa_kernel(
                 in1=second[:, :, :, ::-1],
                 op=ALU.add,
             )
-            nc.sync.dma_start(out=outs[w][a][:, cols], in_=rotated[:, cols])
 
-        def store_v(engine, a, b):
+        def store_rotated(w, a, heads):
+            cols = slice(heads.start * HEAD, heads.stop * HEAD)
+            nc.sync.dma_start(out=outs[w][a][:, cols], in_=state[(w, a)][4][:, cols])
+
+        plain_of = {}
+
+        def copy_v(a, b):
             plain = work.tile([P, BANK], F32, bufs=TOKEN_TILES * BANKS)
-            if engine == "scalar":
-                nc.scalar.copy(out=plain[:], in_=acc_of[(NORMED, a, b)][:])
-            else:
-                nc.vector.tensor_copy(out=plain[:], in_=acc_of[(NORMED, a, b)][:])
-            nc.sync.dma_start(
-                out=outs[NORMED][a][:, b * BANK : (b + 1) * BANK], in_=plain[:]
-            )
+            plain_of[(a, b)] = plain
+            nc.scalar.copy(out=plain[:], in_=acc_of[(NORMED, a, b)][:])
 
-        def both(j):
-            regroup("scalar", j)
-            regroup("vector", j)
+        def store_v(a, b):
+            nc.sync.dma_start(out=outs[NORMED][a][:, b * BANK : (b + 1) * BANK], in_=plain_of[(a, b)][:])
 
         tiles = [(w, a) for w in range(NORMED) for a in range(TOKEN_TILES)]
 
-        def rotate_pair(w):
-            invert(w, 0)
-            rotary_products(w, 0, 0)
-            invert(w, 1)
-            rotary_products(w, 0, 1)
-            for b in range(BANKS):
-                rotary_products(w, 1, b)
-            add_and_store(nc.gpsimd, w, 0, whole)
-
-        def norm(w, a):
-            open_tile(w, a)
-            for b in range(BANKS):
+        def squares(n, banks=range(BANKS)):
+            w, a = tiles[n]
+            if (w, a) not in state:
+                open_tile(w, a)
+            for b in banks:
                 sums_of_squares(w, a, b)
-            root(w, a)
 
-        whole = slice(0, BANKS)
-        sign_sin()
+        def inverse_root(n):
+            root(*tiles[n])
+
+        def products(n, b):
+            rotary_products(*tiles[n], b)
+
+        def add(n, first, last, engine=nc.gpsimd):
+            add_heads(engine, *tiles[n], slice(first, last))
+
+        def store(n, first, last):
+            store_rotated(*tiles[n], slice(first, last))
+
         spread_gains()
+        regroup("vector", 0, 0)
+        sign_sin()
+        build_tables(0)
+        regroup("vector", 0, 1)
+        build_tables(1)
+        regroup("scalar", 0, 0)
+        regroup("scalar", 0, 1)
         for a in range(TOKEN_TILES):
             transpose_x(a)
-        for w in range(NORMED):
-            build_tables(w)
-        both(0)
-        quantise_x()
-        both(1)
         quantise(0)
+        quantise_x()
+        regroup("scalar", 1)
+        regroup("vector", 1)
         multiply(0)
-        both(2)
+        regroup("scalar", 2)
+        regroup("vector", 2)
         quantise(1)
         multiply(1)
-        for a in range(TOKEN_TILES):
-            norm(0, a)
-        both(3)
+        squares(0)
+        regroup("scalar", 3)
+        inverse_root(0)
+        regroup("vector", 3)
         quantise(2)
         multiply(2)
-        rotate_pair(0)
-        both(4)
+        squares(1)
+        regroup("vector", 4)
+        products(0, 0)
         quantise(3)
+        products(0, 1)
         multiply(3)
-        add_and_store(nc.vector, 0, 1, whole)
-        both(5)
-        for a in range(TOKEN_TILES):
-            norm(1, a)
+        add(0, 0, 4)
+        store(0, 0, 4)
+        regroup("scalar", 4, last=128)
+        inverse_root(1)
+        regroup("scalar", 4, first=128)
+        regroup("vector", 5)
+        regroup("scalar", 5)
+        products(1, 0)
+        add(0, 4, 8)
+        store(0, 4, 8)
         quantise(4)
-        multiply(4)
+        multiply(4, [0])
         quantise(5)
-        multiply(5)
-        for b in range(TOKEN_TILES * BANKS):
-            store_v("scalar", *divmod(b, BANKS))
-        rotate_pair(1)
-        for b in range(BANKS):
-            add_and_store(nc.vector, 1, 1, slice(b, b + 1))
+        multiply(5, [0])
+        products(1, 1)
+        squares(2)
+        squares(3, [0])
+        inverse_root(2)
+        squares(3, [1])
+        copy_v(0, 0)
+        store_v(0, 0)
+        inverse_root(3)
+        copy_v(0, 1)
+        store_v(0, 1)
+        add(1, 0, 5)
+        store(1, 0, 5)
+        for j in (4, 5):
+            multiply(j, [1])
+        products(2, 0)
+        add(1, 5, 8)
+        copy_v(1, 0)
+        store_v(1, 0)
+        copy_v(1, 1)
+        store_v(1, 1)
+        store(1, 5, 8)
+        products(2, 1)
+        add(2, 0, 4)
+        store(2, 0, 4)
+        products(3, 0)
+        add(2, 4, 8)
+        store(2, 4, 8)
+        products(3, 1)
+        add(3, 0, 4)
+        store(3, 0, 4)
+        add(3, 4, 7, nc.vector)
+        store(3, 4, 7)
+        add(3, 7, 8, nc.vector)
+        store(3, 7, 8)

@@ -30,8 +30,8 @@ NORMED = 2
 SLABS = 3 * PASSES
 RUN = 8
 PROJ = [0,1,2]
-SCALAR_COLS = [576,448,576,256,512,640]
-PARTS = [2,1,1,1,1,1]
+SCALAR_COLS = [512,576,576,256,576,640]
+PARTS = [1,1,1,1,1,1]
 
 FLOPS = 2 * TOKENS * D_MODEL * 3 * INNER
 
@@ -80,12 +80,10 @@ def tile_flux2parallelselfattention_pa_kernel(
         warm = keep.tile([P, 1], F32)
         nc.scalar.activation(out=warm[:], in_=eps_sb[:], func=ACT.Abs_reciprocal_sqrt)
 
-        load_slab(0, [0])
         nc.sync.dma_start(out=cos_sb[:], in_=cos.rearrange("(p a) i -> p a i", p=P))
         nc.sync.dma_start(out=sin_sb[:], in_=sin.rearrange("(p a) i -> p a i", p=P))
-        load_slab(0, [1])
         nc.sync.dma_start(out=x_sb[:].rearrange("p a k -> p (a k)"), in_=x_rows)
-        for j in range(1, SLABS):
+        for j in range(SLABS):
             load_slab(j)
 
         w_codes = [keep.tile([P, INNER], U32, name="codes%d" % j, align_bytes=64) for j in range(SLABS)]
@@ -200,11 +198,11 @@ def tile_flux2parallelselfattention_pa_kernel(
             rotated = work.tile([P, INNER], F32)
             state[(w, a)] = (squares, sum_sq, inv_rms, terms, rotated)
 
-        def rotary_products(w, a, b):
+        def rotary_products(w, a, first, last):
             inv_rms, terms = state[(w, a)][2:4]
             shape = [P, 2, HEAD]
-            for h in range(HEADS_PER_BANK):
-                head = b * HEADS_PER_BANK + h
+            for head in range(first, last):
+                b, h = divmod(head, HEADS_PER_BANK)
                 nc.vector.scalar_tensor_tensor(
                     out=terms[:, head, :, :],
                     in0=acc_of[(w, a, b)][:, h * HEAD : (h + 1) * HEAD].unsqueeze(1).to_broadcast(shape),
@@ -269,8 +267,8 @@ def tile_flux2parallelselfattention_pa_kernel(
         def inverse_root(n):
             root(*tiles[n])
 
-        def products(n, b):
-            rotary_products(*tiles[n], b)
+        def products(n, first, last):
+            rotary_products(*tiles[n], first, last)
 
         def add(n, first, last, engine=nc.gpsimd):
             add_heads(engine, *tiles[n], slice(first, last))
@@ -279,19 +277,17 @@ def tile_flux2parallelselfattention_pa_kernel(
             store_rotated(*tiles[n], slice(first, last))
 
         spread_gains()
-        regroup("vector", 0, 0)
-        sign_sin()
-        build_tables(0)
-        regroup("vector", 0, 1)
-        build_tables(1)
-        regroup("scalar", 0, 0)
-        regroup("scalar", 0, 1)
         for a in range(TOKEN_TILES):
             transpose_x(a)
-        quantise(0)
+        sign_sin()
+        for w in range(NORMED):
+            build_tables(w)
         quantise_x()
+        regroup("scalar", 0)
+        regroup("vector", 0)
         regroup("scalar", 1)
         regroup("vector", 1)
+        quantise(0)
         multiply(0)
         regroup("scalar", 2)
         regroup("vector", 2)
@@ -305,25 +301,26 @@ def tile_flux2parallelselfattention_pa_kernel(
         multiply(2)
         squares(1)
         regroup("vector", 4)
-        products(0, 0)
         quantise(3)
-        products(0, 1)
         multiply(3)
+        products(0, 0, 4)
+        products(0, 4, 8)
         add(0, 0, 4)
         store(0, 0, 4)
+        add(0, 4, 8)
+        store(0, 4, 8)
         regroup("scalar", 4, last=128)
         inverse_root(1)
         regroup("scalar", 4, first=128)
-        regroup("vector", 5)
         regroup("scalar", 5)
-        products(1, 0)
-        add(0, 4, 8)
-        store(0, 4, 8)
+        products(1, 0, 6)
+        regroup("vector", 5)
         quantise(4)
         multiply(4, [0])
         quantise(5)
         multiply(5, [0])
-        products(1, 1)
+        products(1, 6, 8)
+        add(1, 0, 8)
         squares(2)
         squares(3, [0])
         inverse_root(2)
@@ -333,25 +330,18 @@ def tile_flux2parallelselfattention_pa_kernel(
         inverse_root(3)
         copy_v(0, 1)
         store_v(0, 1)
-        add(1, 0, 5)
-        store(1, 0, 5)
+        store(1, 0, 8)
         for j in (4, 5):
             multiply(j, [1])
-        products(2, 0)
-        add(1, 5, 8)
+        products(2, 0, 8)
         copy_v(1, 0)
         store_v(1, 0)
         copy_v(1, 1)
         store_v(1, 1)
-        store(1, 5, 8)
-        products(2, 1)
-        add(2, 0, 4)
-        store(2, 0, 4)
-        products(3, 0)
-        add(2, 4, 8)
-        store(2, 4, 8)
-        products(3, 1)
-        add(3, 0, 4)
+        add(2, 0, 8)
+        store(2, 0, 8)
+        products(3, 0, 8)
+        add(3, 0, 4, nc.vector)
         store(3, 0, 4)
         add(3, 4, 7, nc.vector)
         store(3, 4, 7)

from contextlib import ExitStack

import concourse.mybir as mybir
from concourse.masks import make_identity

F32 = mybir.dt.float32
BF16 = mybir.dt.bfloat16
U32 = mybir.dt.uint32
U8 = mybir.dt.uint8
FP8X4 = mybir.dt.float8_e4m3fn_x4
ACT = mybir.ActivationFunctionType
ALU = mybir.AluOpType

P = 128
PACK = 4
K_PASS = P * PACK
TOKENS = 256
D_MODEL = 1024
INNER = 1024
HEAD = 128
HALF = HEAD // 2
EPS = 1e-5
BANK = 512
TOKEN_TILES = TOKENS // P
PASSES = D_MODEL // K_PASS
BANKS = INNER // BANK
HEADS_PER_BANK = BANK // HEAD
HEADS = INNER // HEAD
NORMED = 2
SLABS = 3 * PASSES
RUN = 8
PROJ = [0,1,2]
SCALAR_COLS = [512,576,576,256,576,640]
PARTS = [1,1,1,1,1,1]

FLOPS = 2 * TOKENS * D_MODEL * 3 * INNER


def tile_flux2parallelselfattention_pa_kernel(
    tc, hidden_states, w_q, w_k, w_v, norm_q_w, norm_k_w, cos, sin, out_0, out_1, out_2
):
    nc = tc.nc
    weights = [w_q, w_k, w_v]
    gains = [norm_q_w, norm_k_w]
    outs = [o.rearrange("b (p a) h d -> a (b p) (h d)", a=TOKEN_TILES) for o in (out_0, out_1, out_2)]
    x_rows = hidden_states.rearrange("b (p a) k -> (b p) (a k)", a=TOKEN_TILES)

    with ExitStack() as ctx:
        keep = ctx.enter_context(tc.tile_pool(name="keep", bufs=1))
        stage = ctx.enter_context(tc.tile_pool(name="stage", bufs=3))
        work = ctx.enter_context(tc.tile_pool(name="work", bufs=4))
        psum = ctx.enter_context(tc.psum_pool(name="psum", bufs=1))
        ctx.enter_context(tc.manual_schedule())

        raw = [
            [keep.tile([P, PACK // PARTS[j], INNER], BF16, name="raw%d_%d" % (j, u)) for u in range(PARTS[j])]
            for j in range(SLABS)
        ]

        def load_slab(j, parts=None):
            w, c = PROJ[j // PASSES], j % PASSES
            rows = weights[w][c * K_PASS : (c + 1) * K_PASS, :].rearrange("(p t) n -> p t n", t=PACK)
            depth = PACK // PARTS[j]
            for u in range(PARTS[j]) if parts is None else parts:
                nc.sync.dma_start(out=raw[j][u][:], in_=rows[:, u * depth : (u + 1) * depth, :])

        x_sb = keep.tile([P, TOKEN_TILES, D_MODEL], BF16)
        cos_sb = keep.tile([P, TOKEN_TILES, HALF], BF16)
        sin_sb = keep.tile([P, TOKEN_TILES, HALF], BF16)
        gain_cols = [keep.tile([P, 1], BF16, name="gain%d" % w) for w in range(NORMED)]

        ident = keep.tile([P, P], F32)
        make_identity(nc, ident[:])
        eps_sb = keep.tile([P, 1], F32)
        nc.vector.memset(eps_sb[:], EPS)
        ident_bf = keep.tile([P, P], BF16)
        make_identity(nc, ident_bf[:])
        for w in range(NORMED):
            nc.scalar.dma_start(out=gain_cols[w][:], in_=gains[w].unsqueeze(1))
        warm = keep.tile([P, 1], F32)
        nc.scalar.activation(out=warm[:], in_=eps_sb[:], func=ACT.Abs_reciprocal_sqrt)

        nc.sync.dma_start(out=cos_sb[:], in_=cos.rearrange("(p a) i -> p a i", p=P))
        nc.sync.dma_start(out=sin_sb[:], in_=sin.rearrange("(p a) i -> p a i", p=P))
        nc.sync.dma_start(out=x_sb[:].rearrange("p a k -> p (a k)"), in_=x_rows)
        for j in range(SLABS):
            load_slab(j)

        w_codes = [keep.tile([P, INNER], U32, name="codes%d" % j, align_bytes=64) for j in range(SLABS)]
        w_scales = [keep.tile([P, INNER], U8, name="scales%d" % j, align_bytes=64) for j in range(SLABS)]
        grouped_of = {}

        def regroup(engine, j, part=None, first=0, last=INNER):
            if j not in grouped_of:
                grouped = stage.tile([P, INNER, PACK], BF16, align_bytes=64)
                grouped_of[j] = grouped
            split = SCALAR_COLS[j]
            for u in range(PARTS[j]) if part is None else [part]:
                if engine == "scalar":
                    regroup_columns(nc.scalar.copy, j, u, first, min(last, split))
                else:
                    regroup_columns(nc.vector.tensor_copy, j, u, max(first, split), last)

        def regroup_columns(copy, j, u, first, last):
            if first < last:
                depth = PACK // PARTS[j]
                copy(
                    out=grouped_of[j][:, first:last, u * depth : (u + 1) * depth].rearrange("p (g i) t -> p g t i", i=RUN),
                    in_=raw[j][u][:, :, first:last].rearrange("p t (g i) -> p g t i", i=RUN),
                )

        def quantise(j, first=0, last=INNER):
            nc.vector.quantize_mx(
                out=w_codes[j][:, first:last].bitcast(FP8X4),
                scales=w_scales[j][:, first:last],
                in_=grouped_of[j][:, first:last, :].rearrange("p n t -> p (n t)"),
            )

        x_grouped = keep.tile([P, PASSES * TOKENS * PACK], BF16, align_bytes=64)
        x_grouped_words = x_grouped[:].bitcast(F32).rearrange(
            "p (c a s u) -> p c a s u", c=PASSES, a=TOKEN_TILES, s=P, u=2
        )
        x_codes = keep.tile([P, PASSES * TOKENS], U32, align_bytes=64)
        x_scales = keep.tile([P, PASSES * TOKENS], U8, align_bytes=64)

        def transpose_x(a):
            x_words = x_sb[:, a, :].bitcast(F32).rearrange("s (c q u) -> s c u q", c=PASSES, q=P, u=2)
            x_t = psum.tile([P, PASSES, 2, P], F32, tag="bank%d" % (5 + a))
            for c in range(PASSES):
                for u in range(2):
                    nc.tensor.transpose(out=x_t[:, c, u, :], in_=x_words[:, c, u, :], identity=ident[:])
            nc.scalar.copy(
                out=x_grouped_words[:, :, a, :, :], in_=x_t[:].rearrange("p c u s -> p c s u")
            )

        def quantise_x():
            nc.vector.quantize_mx(
                out=x_codes[:].bitcast(FP8X4), scales=x_scales[:], in_=x_grouped[:]
            )

        acc_of = {}

        def multiply(j, tokens=range(TOKEN_TILES)):
            w, c = PROJ[j // PASSES], j % PASSES
            for a in tokens:
                x_cols = slice((c * TOKEN_TILES + a) * P, (c * TOKEN_TILES + a + 1) * P)
                for b in range(BANKS):
                    n_cols = slice(b * BANK, (b + 1) * BANK)
                    if c == 0:
                        at = (PROJ.index(w) % 2 * TOKEN_TILES + a) * BANKS + b
                        acc_of[(w, a, b)] = psum.tile([P, BANK], F32, tag="bank%d" % at, name="acc")
                    nc.tensor.matmul_mx(
                        out=acc_of[(w, a, b)][:],
                        lhsT=x_codes[:, x_cols].bitcast(FP8X4),
                        lhsT_scale=x_scales[:, x_cols],
                        rhs=w_codes[j][:, n_cols].bitcast(FP8X4),
                        rhs_scale=w_scales[j][:, n_cols],
                        start=(c == 0),
                        stop=(c == PASSES - 1),
                    )

        table = [keep.tile([P, TOKEN_TILES, 2, HALF, 2], F32, name="table%d" % w) for w in range(NORMED)]
        signed_sin = keep.tile([P, TOKEN_TILES, HALF, 2], BF16)
        gain_ps = psum.tile([P, NORMED, HEAD], F32, tag="bank4")

        def spread_gains():
            for w in range(NORMED):
                nc.tensor.matmul(
                    out=gain_ps[:, w, :],
                    lhsT=gain_cols[w][:].to_broadcast([P, P]),
                    rhs=ident_bf[:],
                    start=True,
                    stop=True,
                )

        def sign_sin():
            nc.vector.tensor_copy(out=signed_sin[:, :, :, 0], in_=sin_sb[:])
            nc.vector.tensor_scalar_mul(out=signed_sin[:, :, :, 1], in0=sin_sb[:], scalar1=-1.0)

        def build_tables(w):
            gain_pairs = gain_ps[:, w, :].rearrange("p (i e) -> p i e", e=2)
            full = [P, TOKEN_TILES, HALF, 2]
            for x, factor in enumerate((cos_sb[:].unsqueeze(3).to_broadcast(full), signed_sin[:])):
                nc.vector.tensor_tensor(
                    out=table[w][:, :, x, :, :],
                    in0=factor,
                    in1=gain_pairs.unsqueeze(1).to_broadcast(full),
                    op=ALU.mult,
                )

        state = {}

        def open_tile(w, a):
            squares = work.tile([P, INNER], F32)
            sum_sq = work.tile([P, HEADS], F32)
            inv_rms = work.tile([P, HEADS], F32)
            terms = work.tile([P, HEADS, 2, HEAD], F32)
            rotated = work.tile([P, INNER], F32)
            state[(w, a)] = (squares, sum_sq, inv_rms, terms, rotated)

        def rotary_products(w, a, first, last):
            inv_rms, terms = state[(w, a)][2:4]
            shape = [P, 2, HEAD]
            for head in range(first, last):
                b, h = divmod(head, HEADS_PER_BANK)
                nc.vector.scalar_tensor_tensor(
                    out=terms[:, head, :, :],
                    in0=acc_of[(w, a, b)][:, h * HEAD : (h + 1) * HEAD].unsqueeze(1).to_broadcast(shape),
                    scalar=inv_rms[:, head : head + 1],
                    in1=table[w][:, a, :, :, :].rearrange("p x i e -> p x (i e)"),
                    op0=ALU.mult,
                    op1=ALU.mult,
                )

        def sums_of_squares(w, a, b):
            squares, sum_sq = state[(w, a)][0:2]
            for h in range(HEADS_PER_BANK):
                head = b * HEADS_PER_BANK + h
                nc.scalar.activation(
                    out=squares[:, head * HEAD : (head + 1) * HEAD],
                    in_=acc_of[(w, a, b)][:, h * HEAD : (h + 1) * HEAD],
                    func=ACT.Square,
                    accum_out=sum_sq[:, head : head + 1],
                )

        def root(w, a):
            sum_sq, inv_rms = state[(w, a)][1:3]
            nc.scalar.activation(
                out=inv_rms[:], in_=sum_sq[:], func=ACT.Abs_reciprocal_sqrt, bias=eps_sb[:, 0:1], scale=1.0 / HEAD
            )

        def add_heads(engine, w, a, heads):
            terms, rotated = state[(w, a)][3:5]
            cols = slice(heads.start * HEAD, heads.stop * HEAD)
            first = terms[:, heads, 0, :].rearrange("p h (i e) -> p h i e", e=2)
            second = terms[:, heads, 1, :].rearrange("p h (i e) -> p h i e", e=2)
            engine.tensor_tensor(
                out=rotated[:, cols].rearrange("p (h i e) -> p h i e", i=HALF, e=2),
                in0=first,
                in1=second[:, :, :, ::-1],
                op=ALU.add,
            )

        def store_rotated(w, a, heads):
            cols = slice(heads.start * HEAD, heads.stop * HEAD)
            nc.sync.dma_start(out=outs[w][a][:, cols], in_=state[(w, a)][4][:, cols])

        plain_of = {}

        def copy_v(a, b):
            plain = work.tile([P, BANK], F32, bufs=TOKEN_TILES * BANKS)
            plain_of[(a, b)] = plain
            nc.scalar.copy(out=plain[:], in_=acc_of[(NORMED, a, b)][:])

        def store_v(a, b):
            nc.sync.dma_start(out=outs[NORMED][a][:, b * BANK : (b + 1) * BANK], in_=plain_of[(a, b)][:])

        tiles = [(w, a) for w in range(NORMED) for a in range(TOKEN_TILES)]

        def squares(n, banks=range(BANKS)):
            w, a = tiles[n]
            if (w, a) not in state:
                open_tile(w, a)
            for b in banks:
                sums_of_squares(w, a, b)

        def inverse_root(n):
            root(*tiles[n])

        def products(n, first, last):
            rotary_products(*tiles[n], first, last)

        def add(n, first, last, engine=nc.gpsimd):
            add_heads(engine, *tiles[n], slice(first, last))

        def store(n, first, last):
            store_rotated(*tiles[n], slice(first, last))

        spread_gains()
        for a in range(TOKEN_TILES):
            transpose_x(a)
        sign_sin()
        for w in range(NORMED):
            build_tables(w)
        quantise_x()
        regroup("scalar", 0)
        regroup("vector", 0)
        regroup("scalar", 1)
        regroup("vector", 1)
        quantise(0)
        multiply(0)
        regroup("scalar", 2)
        regroup("vector", 2)
        quantise(1)
        multiply(1)
        squares(0)
        regroup("scalar", 3)
        inverse_root(0)
        regroup("vector", 3)
        quantise(2)
        multiply(2)
        squares(1)
        regroup("vector", 4)
        quantise(3)
        multiply(3)
        products(0, 0, 4)
        products(0, 4, 8)
        add(0, 0, 4)
        store(0, 0, 4)
        add(0, 4, 8)
        store(0, 4, 8)
        regroup("scalar", 4, last=128)
        inverse_root(1)
        regroup("scalar", 4, first=128)
        regroup("scalar", 5)
        products(1, 0, 6)
        regroup("vector", 5)
        quantise(4)
        multiply(4, [0])
        quantise(5)
        multiply(5, [0])
        products(1, 6, 8)
        add(1, 0, 8)
        squares(2)
        squares(3, [0])
        inverse_root(2)
        squares(3, [1])
        copy_v(0, 0)
        store_v(0, 0)
        inverse_root(3)
        copy_v(0, 1)
        store_v(0, 1)
        store(1, 0, 8)
        for j in (4, 5):
            multiply(j, [1])
        products(2, 0, 8)
        copy_v(1, 0)
        store_v(1, 0)
        copy_v(1, 1)
        store_v(1, 1)
        add(2, 0, 8)
        store(2, 0, 8)
        products(3, 0, 8)
        add(3, 0, 4, nc.vector)
        store(3, 0, 4)
        add(3, 4, 7, nc.vector)
        store(3, 4, 7)
        add(3, 7, 8, nc.vector)
        store(3, 7, 8)
